import numpy as np
import ml_dtypes


def mxq(x, axis, fmt="e4m3"):
    dtype, down = {"e4m3": (ml_dtypes.float8_e4m3fn, 7), "e5m2": (ml_dtypes.float8_e5m2, 14)}[fmt]
    v = np.moveaxis(np.asarray(x, np.float32).astype(ml_dtypes.bfloat16).astype(np.float64), axis, -1)
    blocks = v.reshape(v.shape[:-1] + (-1, 32))
    amax = np.abs(blocks).max(-1, keepdims=True)
    byte = np.maximum(np.where(amax > 0, np.frexp(amax)[1] - 1 + 127, 0) - down, 1)
    scale = np.exp2(byte - 127.0)
    codes = (blocks / scale).astype(np.float32).astype(dtype).astype(np.float64)
    return np.moveaxis((codes * scale).reshape(v.shape), -1, axis)


WIDE = False


def mx_kscale(k):
    if not WIDE:
        return np.ones(k)
    levels = np.array([10, -10, 5, -5, 0])
    if k % 512:
        return np.exp2(np.random.permutation(np.resize(levels, k // 32))).repeat(32)
    a = np.empty((k // 512, 16))
    for p in range(k // 512):
        a[p, :8] = np.random.permutation(np.resize(levels, 8))
        for g in range(8):
            far = levels[np.abs(levels - a[p, g]) >= 10]
            a[p, g + 8] = far[np.random.randint(len(far))]
    return np.exp2(a.ravel()).repeat(32)


BF16 = ml_dtypes.bfloat16


def bf(x):
    return np.asarray(x, np.float32).astype(BF16)


def f64(x):
    return np.asarray(x).astype(np.float64)


B, N, D, H, Z = 2, 512, 1024, 2, 512
NEG_INF = -1.0e9
CW = 1.3 / Z ** 0.25


def draw0():
    s, t = mx_kscale(D), mx_kscale(Z)
    g1 = np.random.standard_normal((H, Z, D))
    g2 = np.random.standard_normal((H, Z, D))
    return {"x": bf(np.random.standard_normal((B, N, D)) * s),
            "wk": bf((0.25 * g1 + g2) * CW / np.sqrt(D) / s / t[None, :, None]),
            "wq": bf(g1 * CW / np.sqrt(D) / s * t[None, :, None]),
            "betas": bf(1.5 + 0.15 * np.random.standard_normal(H))}


def core(x, wk, wq, betas):
    beta = f64(betas)
    xq = mxq(f64(x).reshape(B * N, D), 1, "e4m3")
    k = (xq @ mxq(f64(wk).reshape(H * Z, D), 1, "e4m3").T).reshape(B, N, H, Z).transpose(0, 2, 1, 3)
    q = (xq @ mxq(f64(wq).reshape(H * Z, D), 1, "e4m3").T).reshape(B, N, H, Z).transpose(0, 2, 1, 3)
    a = beta[None, :, None, None] * (mxq(q, 3, "e4m3") @ mxq(k, 3, "e4m3").transpose(0, 1, 3, 2))
    a = np.where(np.eye(N, dtype=bool)[None, None], NEG_INF, a)
    top = a.max(-1, keepdims=True)
    lse = top[..., 0] + np.log(np.exp(a - top).sum(-1))
    return -(lse / beta[None, :, None])


def e4m3fn_bytes(y):
    return np.clip(np.asarray(y, np.float64), -448.0, 448.0).astype(np.float32).astype(ml_dtypes.float8_e4m3fn).view(np.uint8)


def e4m3fn_values(b):
    return np.asarray(b, np.uint8).view(ml_dtypes.float8_e4m3fn).astype(np.float64)


def setup_inputs():
    d = draw0()
    x0 = np.asarray(d['x']).astype(np.float64)
    s = (np.max(np.abs(x0), axis=(0, 1), keepdims=True) / 448.0).astype(np.float32)
    out = {}
    for k, v in d.items():
        if k == 'x':
            out['x_bytes'] = e4m3fn_bytes(x0 / s.astype(np.float64))
            out['x_scale'] = s
        else:
            out[k] = v
    return out


def reference(x_bytes, x_scale, wk, wq, betas):
    return core(e4m3fn_values(x_bytes) * x_scale.astype(np.float64), wk, wq, betas)

@@ -1,0 +1,316 @@
+from contextlib import ExitStack
+
+import concourse.mybir as mybir
+from concourse.masks import make_identity
+
+B, N, D, H, Z = 2, 512, 1024, 2, 512
+P = 128
+PASSES = D // 512
+TB = N // P
+FLOPS = 2 * (2 * B * N * D * H * Z) + 2 * B * H * N * N * Z
+NEG = -1.0e9
+
+ORDER = (
+    "k00 k01 k02 k03 x00 x01 q00 q01 x02 q02 q03 x03 "
+    "k10 k11 k12 k13 K000 K001 K002 K003 q10 q11 q12 q13 Q000 Q001 Q002 Q003 "
+    "x10 x11 K010 K011 S000 S001 K012 K013 x12 x13 Q010 Q011 S002 S003 Q012 Q013 "
+    "K100 K101 S010 S011 K102 K103 Q100 Q101 S012 S013 Q102 Q103 "
+    "K110 K111 S100 S101 K112 K113 Q110 S102 S103 Q111 Q112 S110 Q113 S111 S112 S113"
+)
+LAG = {"X": 3.55, "Q": 5.45, "A": 3.65, "R": 4.25, "G": 4.35, "B": 5.15, "E": 8.15, "F": 7.15}
+MULT0, MULT_STEP, MULT4 = -1, 1.5, 23
+V_FIRST, V_LAST, V_STEP = 8, 30, 4
+
+F32 = mybir.dt.float32
+BF16 = mybir.dt.bfloat16
+U32 = mybir.dt.uint32
+U8 = mybir.dt.uint8
+F8 = mybir.dt.float8_e4m3fn
+X4 = mybir.dt.float8_e4m3fn_x4
+ALU = mybir.AluOpType
+ACT = mybir.ActivationFunctionType
+AX = mybir.AxisListType
+
+
+def tile_multiheadenergyattention_pa_kernel(tc, x_bytes, x_scale, wk, wq, betas, out):
+    nc = tc.nc
+    weights = {"k": wk, "q": wq}
+    with ExitStack() as ctx:
+        keep = ctx.enter_context(tc.tile_pool(name="keep", bufs=1))
+        ring = ctx.enter_context(tc.tile_pool(name="ring", bufs=6))
+        psum = ctx.enter_context(tc.psum_pool(name="psum", bufs=4))
+        ctx.enter_context(tc.manual_schedule())
+
+        xbytes = {}
+        wrows = {}
+
+        def load_x(b, lo, hi):
+            t = keep.tile([P, hi - lo, D], U8, name="xbytes%d%d" % (b, lo), align_bytes=64)
+            nc.sync.dma_start(out=t[:], in_=x_bytes[b, lo * P : hi * P, :].rearrange("(j p) d -> p j d", p=P))
+            for j in range(lo, hi):
+                xbytes[b, j] = t[:, j - lo, :]
+
+        def load_w(m, h, lo, hi):
+            t = keep.tile([P, hi - lo, D], BF16, name="w%s%d%d" % (m, h, lo), align_bytes=64)
+            nc.sync.dma_start(out=t[:], in_=weights[m][h].rearrange("(z t) d -> z t d", t=4)[:, lo:hi, :])
+            for i in range(lo, hi):
+                wrows[h, m, i] = t[:, i - lo, :]
+
+        load_w("k", 0, 0, 1)
+        load_w("k", 0, 1, 2)
+        scale_t = keep.tile([P, D], F32, name="scale_t", align_bytes=64)
+        nc.sync.dma_start(out=scale_t[:], in_=x_scale.rearrange("a b k -> (a b k)").partition_broadcast(P))
+        load_x(0, 0, 2)
+        load_w("k", 0, 2, 4)
+        load_x(0, 2, 4)
+        load_w("q", 0, 0, 2)
+        beta_b = keep.tile([P, H], BF16, name="beta_b", align_bytes=64)
+        nc.sync.dma_start(out=beta_b[:], in_=betas.partition_broadcast(P))
+        load_w("q", 0, 2, 4)
+        load_w("k", 1, 0, 2)
+        load_w("k", 1, 2, 4)
+        load_x(1, 0, 4)
+        load_w("q", 1, 0, 2)
+        load_w("q", 1, 2, 4)
+
+        one = keep.tile([P, 1], F32, name="one", align_bytes=64)
+        nc.gpsimd.memset(one[:], 1.0)
+        junk1 = keep.tile([P, 1], F32, name="junk1", align_bytes=64)
+        nc.scalar.activation(out=junk1[:], in_=one[:], func=ACT.Exp)
+        ident = keep.tile([P, P], F32, name="ident", align_bytes=64)
+        make_identity(nc, ident[:])
+        mask = keep.tile([P, P], F32, name="mask", align_bytes=64)
+        nc.gpsimd.tensor_scalar(out=mask[:], in0=ident[:], scalar1=NEG, scalar2=0.0, op0=ALU.mult, op1=ALU.add)
+        nbt = keep.tile([P, P], F32, name="nbt", align_bytes=64)
+        nc.gpsimd.memset(nbt[:], 0.0)
+        tot = keep.tile([P, P], F32, name="tot", align_bytes=64)
+        nc.gpsimd.memset(tot[:], 0.0)
+        ibc = keep.tile([P, P], F32, name="ibc", align_bytes=64)
+        nc.gpsimd.memset(ibc[:], 0.0)
+        beta = keep.tile([P, H], F32, name="beta", align_bytes=64)
+        nbeta = keep.tile([P, H], F32, name="nbeta", align_bytes=64)
+        ib = keep.tile([P, H], F32, name="ib", align_bytes=64)
+        sums = keep.tile([P, 2, 16], F32, name="sums", align_bytes=64)
+        ib16 = keep.tile([16, 2], F32, name="ib16", align_bytes=64)
+
+        codes = {}
+        bank = {}
+        grouped = {}
+        xb = {}
+        cols = {}
+        for b in range(B):
+            for h in range(H):
+                for m in "kq":
+                    cols[b, h, m] = (
+                        keep.tile([P, N], U32, name="c%s%d%d" % (m, b, h), align_bytes=256),
+                        keep.tile([P, N], U8, name="s%s%d%d" % (m, b, h), align_bytes=256),
+                    )
+
+        def mult(b, j):
+            t = ring.tile([P, D], BF16, name="xb", align_bytes=64)
+            nc.vector.tensor_tensor(out=t[:], in0=xbytes[b, j].bitcast(F8), in1=scale_t[:], op=ALU.mult)
+            xb[b, j] = t[:]
+
+        def turn_x(key, b, j):
+            turn(key, xb[b, j])
+
+        def turn_w(key, m, h, t):
+            turn(key, wrows[h, m, t])
+
+        def turn(key, rows):
+            ps = psum.tile([P, 4, P], F32, tag="z", name="turned")
+            words = rows.bitcast(F32)
+            for g in range(PASSES):
+                for u in range(2):
+                    nc.tensor.transpose(ps[:, 2 * g + u, :], words[:, 256 * g + u : 256 * (g + 1) : 2], ident[:])
+            bank[key] = ps
+
+        def take_turn(key):
+            g = ring.tile([P, PASSES, P, 4], BF16, name="gt", align_bytes=64)
+            dst = g[:].rearrange("p g r e -> p (g r e)").bitcast(F32).rearrange("p (g r u) -> p g r u", g=PASSES, u=2)
+            nc.scalar.copy(out=dst, in_=bank[key][:].rearrange("p (g u) r -> p g r u", u=2))
+            grouped[key] = g
+
+        def quant_turn(key):
+            c = keep.tile([P, PASSES, P], U32, name="c_" + key, align_bytes=256)
+            s = keep.tile([P, PASSES, P], U8, name="s_" + key, align_bytes=256)
+            nc.vector.quantize_mx(
+                out=c[:].rearrange("p g r -> p (g r)").bitcast(X4),
+                scales=s[:].rearrange("p g r -> p (g r)"),
+                in_=grouped[key][:].rearrange("p g r e -> p (g r e)"),
+            )
+            codes[key] = (c, s)
+
+        def mm_proj(key, b, h, m, j):
+            ps = psum.tile([P, 4, P], F32, tag="a", name="proj")
+            xc, xs = codes["x%d%d" % (b, j)]
+            for t in range(4):
+                wc, ws = codes["%s%d%d" % (m, h, t)]
+                for g in range(PASSES):
+                    nc.tensor.matmul_mx(
+                        out=ps[:, t, :], lhsT=wc[:, g, :].bitcast(X4), lhsT_scale=ws[:, g, :],
+                        rhs=xc[:, g, :].bitcast(X4), rhs_scale=xs[:, g, :],
+                        start=(g == 0), stop=(g == PASSES - 1),
+                    )
+            bank[key] = ps
+
+        def take_proj(key, on_vector):
+            g = ring.tile([P, P, 4], BF16, name="gp", align_bytes=64)
+            src = bank[key][:].rearrange("p t n -> p n t")
+            if on_vector:
+                nc.vector.tensor_copy(out=g[:], in_=src)
+            else:
+                nc.scalar.copy(out=g[:], in_=src)
+            grouped[key] = g
+
+        def quant_proj(key, b, h, m, j):
+            c, s = cols[b, h, m]
+            nc.vector.quantize_mx(
+                out=c[:, j * P : (j + 1) * P].bitcast(X4), scales=s[:, j * P : (j + 1) * P],
+                in_=grouped[key][:].rearrange("p n t -> p (n t)"),
+            )
+
+        def mm_score(key, b, h, j):
+            ps = psum.tile([P, N], F32, tag="z", name="score")
+            qc, qs = cols[b, h, "q"]
+            kc, ks = cols[b, h, "k"]
+            o = j ^ 1
+            pair = 2 - 2 * (j // 2)
+            for dst, src, w in ((0, j, P), (P, o, P), (2 * P, pair, 2 * P)):
+                nc.tensor.matmul_mx(
+                    out=ps[:, dst : dst + w],
+                    lhsT=qc[:, j * P : (j + 1) * P].bitcast(X4), lhsT_scale=qs[:, j * P : (j + 1) * P],
+                    rhs=kc[:, src * P : src * P + w].bitcast(X4), rhs_scale=ks[:, src * P : src * P + w],
+                    start=True, stop=True,
+                )
+            bank[key] = ps
+
+        peaks = {}
+        diags = {}
+
+        def hide(key):
+            dg = ring.tile([P, P], F32, name="dg", align_bytes=64)
+            nc.vector.tensor_tensor(out=dg[:], in0=bank[key][:, 0:P], in1=mask[:], op=ALU.add)
+            diags[key] = dg
+            peaks[key] = ring.tile([P, 2], F32, name="pk", align_bytes=64)
+
+        def peak_rest(key):
+            nc.vector.reduce_max(out=peaks[key][:, 0:1], in_=bank[key][:, P:N], axis=AX.X)
+
+        def peak_diag(key):
+            nc.vector.reduce_max(out=peaks[key][:, 1:2], in_=diags[key][:], axis=AX.X)
+
+        def bias(key, h, c):
+            pk = peaks[key]
+            nc.vector.scalar_tensor_tensor(
+                out=nbt[:, c : c + 1], in0=pk[:, 0:1], scalar=pk[:, 1:2], in1=nbeta[:, h : h + 1],
+                op0=ALU.max, op1=ALU.mult,
+            )
+
+        def exp_rest(key, h, c):
+            e1 = ring.tile([P, 3 * P], BF16, name="e1", align_bytes=64)
+            nc.scalar.activation(
+                out=e1[:], in_=bank[key][:, P:N], func=ACT.Exp, bias=nbt[:, c : c + 1],
+                scale=beta[:, h : h + 1], accum_out=sums[:, 0, c : c + 1],
+            )
+
+        def exp_diag(key, h, c):
+            e2 = ring.tile([P, P], BF16, name="e2", align_bytes=64)
+            nc.scalar.activation(
+                out=e2[:], in_=diags[key][:], func=ACT.Exp, bias=nbt[:, c : c + 1],
+                scale=beta[:, h : h + 1], accum_out=sums[:, 1, c : c + 1],
+            )
+
+        def setup_beta():
+            nc.vector.tensor_copy(out=beta[:], in_=beta_b[:])
+            nc.vector.tensor_scalar(out=nbeta[:], in0=beta[:], scalar1=-1.0, scalar2=None, op0=ALU.mult)
+            nc.vector.reciprocal(out=ib[:], in_=beta[:])
+            ibv = ibc[:, 0:16].rearrange("p (b h j) -> p b h j", b=B, h=H)
+            for h in range(H):
+                nc.vector.tensor_scalar(
+                    out=ibv[:, :, h, :], in0=ibv[:, :, h, :], scalar1=ib[:, h : h + 1], scalar2=None, op0=ALU.add
+                )
+
+        def turn_beta():
+            pt = psum.tile([P, P], F32, tag="a", name="ibt")
+            nc.tensor.transpose(pt[:], ibc[:], ident[:])
+            bank["beta"] = pt
+
+        def take_beta():
+            pt = bank["beta"]
+            nc.vector.tensor_copy(out=ib16[:, 0:1], in_=pt[0:16, 0:1])
+            nc.vector.tensor_scalar(out=ib16[:, 1:2], in0=pt[0:16, 0:1], scalar1=-1.0, scalar2=None, op0=ALU.mult)
+
+        order = ORDER.split()
+        proj = [t for t in order if t[0] in "KQ"]
+        queues = {"S": [], "V": [], "T": []}
+
+        def add(engine, slot, key, needs, emit, *args):
+            queues[engine].append((slot, len(queues[engine]), key, needs, emit, args))
+
+        xs = [t for t in order if t[0] == "x"]
+        for i, t in enumerate(order):
+            kind, a, c = t[0], int(t[1]), int(t[2])
+            if kind in "kqx":
+                if kind == "x":
+                    n = xs.index(t)
+                    add("V", MULT0 + MULT_STEP * n if n < 4 else MULT4 + n - 4, "M" + t, [], mult, a, c)
+                    add("T", i, "T" + t, ["M" + t], turn_x, t, a, c)
+                else:
+                    add("T", i, "T" + t, [], turn_w, t, kind, a, c)
+                add("S", i + LAG["X"], "X" + t, ["T" + t], take_turn, t)
+                add("V", i + LAG["Q"], "Q" + t, ["X" + t], quant_turn, t)
+            elif kind in "KQ":
+                m, j = {"K": "k", "Q": "q"}[kind], int(t[3])
+                needs = ["Qx%d%d" % (a, j)] + ["Q%s%d%d" % (m, c, z) for z in range(4)]
+                add("T", i, "T" + t, needs, mm_proj, t, a, c, m, j)
+                n = proj.index(t)
+                on_vector = V_FIRST <= n < V_LAST and (n - V_FIRST) % V_STEP == 0
+                add("V" if on_vector else "S", i + LAG["X"], "X" + t, ["T" + t], take_proj, t, on_vector)
+                add("V", i + LAG["Q"], "Q" + t, ["X" + t], quant_proj, t, a, c, m, j)
+            else:
+                j = int(t[3])
+                col = (a * H + c) * TB + j
+                needs = ["QQ%d%d%d" % (a, c, j)] + ["QK%d%d%d" % (a, c, z) for z in range(4)]
+                add("T", i, "T" + t, needs, mm_score, t, a, c, j)
+                add("V", i + LAG["A"], "A" + t, ["T" + t], hide, t)
+                add("V", i + LAG["R"], "R" + t, ["T" + t], peak_rest, t)
+                add("V", i + LAG["G"], "G" + t, ["A" + t], peak_diag, t)
+                add("V", i + LAG["B"], "B" + t, ["R" + t, "G" + t], bias, t, c, col)
+                add("S", i + LAG["E"], "E" + t, ["B" + t], exp_rest, t, c, col)
+                add("S", i + LAG["F"], "F" + t, ["B" + t], exp_diag, t, c, col)
+
+        add("V", 20.5, "beta", [], setup_beta)
+        add("T", 40.5, "turn_beta", ["beta"], turn_beta)
+        add("V", 47.5, "take_beta", ["turn_beta"], take_beta)
+        queues = {e: sorted(queues[e]) for e in "SVT"}
+        done = set()
+        heads = {"S": 0, "V": 0, "T": 0}
+        while any(heads[e] < len(queues[e]) for e in heads):
+            moved = False
+            for e in "SVT":
+                while heads[e] < len(queues[e]):
+                    slot, n, key, needs, emit, args = queues[e][heads[e]]
+                    if not all(k in done for k in needs):
+                        break
+                    emit(*args)
+                    done.add(key)
+                    heads[e] += 1
+                    moved = True
+                    if e == "T":
+                        break
+            assert moved
+
+        fin = psum.tile([P, 2, P], F32, tag="a", name="fin")
+        nc.tensor.transpose(fin[:, 0, :], nbt[:], ident[:])
+        pre = keep.tile([16, P], F32, name="pre", align_bytes=64)
+        nc.vector.tensor_scalar(out=pre[:], in0=fin[0:16, 0, :], scalar1=ib16[:, 0:1], scalar2=None, op0=ALU.mult)
+        nc.vector.tensor_tensor(out=tot[:, 0:16], in0=sums[:, 0, :], in1=sums[:, 1, :], op=ALU.add)
+        nc.tensor.transpose(fin[:, 1, :], tot[:], ident[:])
+        ln = keep.tile([16, P], F32, name="ln", align_bytes=64)
+        nc.scalar.activation(out=ln[:], in_=fin[0:16, 1, :], func=ACT.Ln)
+        res = keep.tile([16, P], F32, name="res", align_bytes=64)
+        nc.vector.scalar_tensor_tensor(
+            out=res[:], in0=ln[:], scalar=ib16[:, 1:2], in1=pre[:], op0=ALU.mult, op1=ALU.add
+        )
+        nc.sync.dma_start(out=out.rearrange("b h (j p) -> (b h j) p", p=P), in_=res[:])

@@ -12,14 +12,15 @@ NEG = -1.0e9
 
 ORDER = (
     "k00 k01 k02 k03 x00 x01 q00 q01 x02 q02 q03 x03 "
-    "k10 k11 k12 k13 K000 K001 K002 K003 q10 q11 q12 q13 Q000 Q001 Q002 Q003 "
+    "K000 K001 K002 K003 k10 k11 k12 k13 Q000 Q001 Q002 Q003 q10 q11 q12 q13 "
     "x10 x11 K010 K011 S000 S001 K012 K013 x12 x13 Q010 Q011 S002 S003 Q012 Q013 "
-    "K100 K101 S010 S011 K102 K103 Q100 Q101 S012 S013 Q102 Q103 "
+    "K100 K101 S010 K102 K103 S011 Q100 Q101 S012 Q102 Q103 S013 "
     "K110 K111 S100 S101 K112 K113 Q110 S102 S103 Q111 Q112 S110 Q113 S111 S112 S113"
 )
-LAG = {"X": 3.55, "Q": 5.45, "A": 3.65, "R": 4.25, "G": 4.35, "B": 5.15, "E": 8.15, "F": 7.15}
-MULT0, MULT_STEP, MULT4 = -1, 1.5, 23
-V_FIRST, V_LAST, V_STEP = 8, 30, 4
+LAG = {"X": 1.75, "Q": 4.25, "A": 2.25, "R": 2.95, "G": 3.05, "B": 3.55, "E": 5.75, "F": 6.55}
+WARM_START, WARM_TASKS, SCALE_SLOT = 5, 12, 0
+MULT0, MULT_STEP, MULT4 = 0, 2.5, 21
+V_FIRST, V_LAST, V_STEP = 11, 30, 4
 
 F32 = mybir.dt.float32
 BF16 = mybir.dt.bfloat16
@@ -56,10 +57,10 @@ def tile_multiheadenergyattention_pa_kernel(tc, x_bytes, x_scale, wk, wq, betas,
             for i in range(lo, hi):
                 wrows[h, m, i] = t[:, i - lo, :]
 
+        sv = keep.tile([P, 2, 4], F32, name="sv", align_bytes=64)
+        nc.sync.dma_start(out=sv[:], in_=x_scale.rearrange("a b (c p m) -> (a b p) c m", c=2, m=4))
         load_w("k", 0, 0, 1)
         load_w("k", 0, 1, 2)
-        scale_t = keep.tile([P, D], F32, name="scale_t", align_bytes=64)
-        nc.sync.dma_start(out=scale_t[:], in_=x_scale.rearrange("a b k -> (a b k)").partition_broadcast(P))
         load_x(0, 0, 2)
         load_w("k", 0, 2, 4)
         load_x(0, 2, 4)
@@ -73,6 +74,9 @@ def tile_multiheadenergyattention_pa_kernel(tc, x_bytes, x_scale, wk, wq, betas,
         load_w("q", 1, 0, 2)
         load_w("q", 1, 2, 4)
 
+        scale_t = keep.tile([P, D], F32, name="scale_t", align_bytes=64)
+        wz = keep.tile([P, N], BF16, name="wz", align_bytes=64)
+        nc.vector.memset(wz[:], 0.0)
         one = keep.tile([P, 1], F32, name="one", align_bytes=64)
         nc.gpsimd.memset(one[:], 1.0)
         junk1 = keep.tile([P, 1], F32, name="junk1", align_bytes=64)
@@ -111,6 +115,21 @@ def tile_multiheadenergyattention_pa_kernel(tc, x_bytes, x_scale, wk, wq, betas,
             nc.vector.tensor_tensor(out=t[:], in0=xbytes[b, j].bitcast(F8), in1=scale_t[:], op=ALU.mult)
             xb[b, j] = t[:]
 
+        def warm(width):
+            ps = psum.tile([P, N], F32, tag="a", name="warmed")
+            nc.tensor.matmul(out=ps[:, 0:width], lhsT=wz[:, 0:P], rhs=wz[:, 0:width], start=True, stop=True)
+
+        def turn_scale():
+            for c in range(2):
+                ps = psum.tile([P, 4, P], F32, tag="z", name="scaled")
+                for m in range(4):
+                    nc.tensor.transpose(ps[:, m, :], sv[:, c, m : m + 1].to_broadcast([P, P]), ident[:])
+                bank["scale%d" % c] = ps
+
+        def take_scale(c, copy):
+            dst = scale_t[:, 512 * c : 512 * (c + 1)].rearrange("p (n m) -> p n m", m=4)
+            copy(out=dst, in_=bank["scale%d" % c][:].rearrange("p m n -> p n m"))
+
         def turn_x(key, b, j):
             turn(key, xb[b, j])
 
@@ -125,10 +144,10 @@ def tile_multiheadenergyattention_pa_kernel(tc, x_bytes, x_scale, wk, wq, betas,
                     nc.tensor.transpose(ps[:, 2 * g + u, :], words[:, 256 * g + u : 256 * (g + 1) : 2], ident[:])
             bank[key] = ps
 
-        def take_turn(key):
+        def take_turn(key, copy):
             g = ring.tile([P, PASSES, P, 4], BF16, name="gt", align_bytes=64)
             dst = g[:].rearrange("p g r e -> p (g r e)").bitcast(F32).rearrange("p (g r u) -> p g r u", g=PASSES, u=2)
-            nc.scalar.copy(out=dst, in_=bank[key][:].rearrange("p (g u) r -> p g r u", u=2))
+            copy(out=dst, in_=bank[key][:].rearrange("p (g u) r -> p g r u", u=2))
             grouped[key] = g
 
         def quant_turn(key):
@@ -231,16 +250,6 @@ def tile_multiheadenergyattention_pa_kernel(tc, x_bytes, x_scale, wk, wq, betas,
                     out=ibv[:, :, h, :], in0=ibv[:, :, h, :], scalar1=ib[:, h : h + 1], scalar2=None, op0=ALU.add
                 )
 
-        def turn_beta():
-            pt = psum.tile([P, P], F32, tag="a", name="ibt")
-            nc.tensor.transpose(pt[:], ibc[:], ident[:])
-            bank["beta"] = pt
-
-        def take_beta():
-            pt = bank["beta"]
-            nc.vector.tensor_copy(out=ib16[:, 0:1], in_=pt[0:16, 0:1])
-            nc.vector.tensor_scalar(out=ib16[:, 1:2], in0=pt[0:16, 0:1], scalar1=-1.0, scalar2=None, op0=ALU.mult)
-
         order = ORDER.split()
         proj = [t for t in order if t[0] in "KQ"]
         queues = {"S": [], "V": [], "T": []}
@@ -254,11 +263,14 @@ def tile_multiheadenergyattention_pa_kernel(tc, x_bytes, x_scale, wk, wq, betas,
             if kind in "kqx":
                 if kind == "x":
                     n = xs.index(t)
-                    add("V", MULT0 + MULT_STEP * n if n < 4 else MULT4 + n - 4, "M" + t, [], mult, a, c)
+                    add("V", MULT0 + MULT_STEP * n if n < 4 else MULT4 + n - 4, "M" + t, ["scale0", "scale1"], mult, a, c)
                     add("T", i, "T" + t, ["M" + t], turn_x, t, a, c)
                 else:
                     add("T", i, "T" + t, [], turn_w, t, kind, a, c)
-                add("S", i + LAG["X"], "X" + t, ["T" + t], take_turn, t)
+                if t in ("x11", "x13"):
+                    add("V", i + LAG["X"], "X" + t, ["T" + t], take_turn, t, nc.vector.tensor_copy)
+                else:
+                    add("S", i + LAG["X"], "X" + t, ["T" + t], take_turn, t, nc.scalar.copy)
                 add("V", i + LAG["Q"], "Q" + t, ["X" + t], quant_turn, t)
             elif kind in "KQ":
                 m, j = {"K": "k", "Q": "q"}[kind], int(t[3])
@@ -280,9 +292,14 @@ def tile_multiheadenergyattention_pa_kernel(tc, x_bytes, x_scale, wk, wq, betas,
                 add("S", i + LAG["E"], "E" + t, ["B" + t], exp_rest, t, c, col)
                 add("S", i + LAG["F"], "F" + t, ["B" + t], exp_diag, t, c, col)
 
+            if i < WARM_TASKS and kind in "kqx":
+                add("T", i + 0.5, "D%d" % i, [], warm, 2 * P)
+        for i in range(WARM_START):
+            add("T", -1.0, "W%d" % i, [], warm, N)
+        add("T", SCALE_SLOT - 0.1, "scale", [], turn_scale)
+        add("S", SCALE_SLOT - 0.1, "scale0", ["scale"], take_scale, 0, nc.scalar.copy)
+        add("V", SCALE_SLOT - 0.1, "scale1", ["scale", "scale0"], take_scale, 1, nc.vector.tensor_copy)
         add("V", 20.5, "beta", [], setup_beta)
-        add("T", 40.5, "turn_beta", ["beta"], turn_beta)
-        add("V", 47.5, "take_beta", ["turn_beta"], take_beta)
         queues = {e: sorted(queues[e]) for e in "SVT"}
         done = set()
         heads = {"S": 0, "V": 0, "T": 0}
@@ -302,13 +319,17 @@ def tile_multiheadenergyattention_pa_kernel(tc, x_bytes, x_scale, wk, wq, betas,
             assert moved
 
         fin = psum.tile([P, 2, P], F32, tag="a", name="fin")
+        nc.tensor.transpose(fin[:, 1, :], ibc[:], ident[:])
         nc.tensor.transpose(fin[:, 0, :], nbt[:], ident[:])
+        nc.vector.tensor_copy(out=ib16[:, 0:1], in_=fin[0:16, 1, 0:1])
+        nc.vector.tensor_scalar(out=ib16[:, 1:2], in0=fin[0:16, 1, 0:1], scalar1=-1.0, scalar2=None, op0=ALU.mult)
+        nc.vector.tensor_tensor(out=tot[:, 0:16], in0=sums[:, 0, :], in1=sums[:, 1, :], op=ALU.add)
+        turned = psum.tile([P, P], F32, tag="z", name="turned_tot")
+        nc.tensor.transpose(turned[:], tot[:], ident[:])
         pre = keep.tile([16, P], F32, name="pre", align_bytes=64)
         nc.vector.tensor_scalar(out=pre[:], in0=fin[0:16, 0, :], scalar1=ib16[:, 0:1], scalar2=None, op0=ALU.mult)
-        nc.vector.tensor_tensor(out=tot[:, 0:16], in0=sums[:, 0, :], in1=sums[:, 1, :], op=ALU.add)
-        nc.tensor.transpose(fin[:, 1, :], tot[:], ident[:])
         ln = keep.tile([16, P], F32, name="ln", align_bytes=64)
-        nc.scalar.activation(out=ln[:], in_=fin[0:16, 1, :], func=ACT.Ln)
+        nc.scalar.activation(out=ln[:], in_=turned[0:16, :], func=ACT.Ln)
         res = keep.tile([16, P], F32, name="res", align_bytes=64)
         nc.vector.scalar_tensor_tensor(
             out=res[:], in0=ln[:], scalar=ib16[:, 1:2], in1=pre[:], op0=ALU.mult, op1=ALU.add

from contextlib import ExitStack

import concourse.mybir as mybir
from concourse.masks import make_identity

B, N, D, H, Z = 2, 512, 1024, 2, 512
P = 128
PASSES = D // 512
TB = N // P
FLOPS = 2 * (2 * B * N * D * H * Z) + 2 * B * H * N * N * Z
NEG = -1.0e9

ORDER = (
    "k00 k01 k02 k03 x00 x01 q00 q01 x02 q02 q03 x03 "
    "K000 K001 K002 K003 k10 k11 k12 k13 Q000 Q001 Q002 Q003 q10 q11 q12 q13 "
    "x10 x11 K010 K011 S000 S001 K012 K013 x12 x13 Q010 Q011 S002 S003 Q012 Q013 "
    "K100 K101 S010 K102 K103 S011 Q100 Q101 S012 Q102 Q103 S013 "
    "K110 K111 S100 S101 K112 K113 Q110 S102 S103 Q111 Q112 S110 Q113 S111 S112 S113"
)
LAG = {"X": 1.75, "Q": 4.25, "A": 2.25, "R": 2.95, "G": 3.05, "B": 3.55, "E": 5.75, "F": 6.55}
WARM_START, WARM_TASKS, SCALE_SLOT = 5, 12, 0
MULT0, MULT_STEP, MULT4 = 0, 2.5, 21
V_FIRST, V_LAST, V_STEP = 11, 30, 4

F32 = mybir.dt.float32
BF16 = mybir.dt.bfloat16
U32 = mybir.dt.uint32
U8 = mybir.dt.uint8
F8 = mybir.dt.float8_e4m3fn
X4 = mybir.dt.float8_e4m3fn_x4
ALU = mybir.AluOpType
ACT = mybir.ActivationFunctionType
AX = mybir.AxisListType


def tile_multiheadenergyattention_pa_kernel(tc, x_bytes, x_scale, wk, wq, betas, out):
    nc = tc.nc
    weights = {"k": wk, "q": wq}
    with ExitStack() as ctx:
        keep = ctx.enter_context(tc.tile_pool(name="keep", bufs=1))
        ring = ctx.enter_context(tc.tile_pool(name="ring", bufs=6))
        psum = ctx.enter_context(tc.psum_pool(name="psum", bufs=4))
        ctx.enter_context(tc.manual_schedule())

        xbytes = {}
        wrows = {}

        def load_x(b, lo, hi):
            t = keep.tile([P, hi - lo, D], U8, name="xbytes%d%d" % (b, lo), align_bytes=64)
            nc.sync.dma_start(out=t[:], in_=x_bytes[b, lo * P : hi * P, :].rearrange("(j p) d -> p j d", p=P))
            for j in range(lo, hi):
                xbytes[b, j] = t[:, j - lo, :]

        def load_w(m, h, lo, hi):
            t = keep.tile([P, hi - lo, D], BF16, name="w%s%d%d" % (m, h, lo), align_bytes=64)
            nc.sync.dma_start(out=t[:], in_=weights[m][h].rearrange("(z t) d -> z t d", t=4)[:, lo:hi, :])
            for i in range(lo, hi):
                wrows[h, m, i] = t[:, i - lo, :]

        sv = keep.tile([P, 2, 4], F32, name="sv", align_bytes=64)
        nc.sync.dma_start(out=sv[:], in_=x_scale.rearrange("a b (c p m) -> (a b p) c m", c=2, m=4))
        load_w("k", 0, 0, 1)
        load_w("k", 0, 1, 2)
        load_x(0, 0, 2)
        load_w("k", 0, 2, 4)
        load_x(0, 2, 4)
        load_w("q", 0, 0, 2)
        beta_b = keep.tile([P, H], BF16, name="beta_b", align_bytes=64)
        nc.sync.dma_start(out=beta_b[:], in_=betas.partition_broadcast(P))
        load_w("q", 0, 2, 4)
        load_w("k", 1, 0, 2)
        load_w("k", 1, 2, 4)
        load_x(1, 0, 4)
        load_w("q", 1, 0, 2)
        load_w("q", 1, 2, 4)

        scale_t = keep.tile([P, D], F32, name="scale_t", align_bytes=64)
        wz = keep.tile([P, N], BF16, name="wz", align_bytes=64)
        nc.vector.memset(wz[:], 0.0)
        one = keep.tile([P, 1], F32, name="one", align_bytes=64)
        nc.gpsimd.memset(one[:], 1.0)
        junk1 = keep.tile([P, 1], F32, name="junk1", align_bytes=64)
        nc.scalar.activation(out=junk1[:], in_=one[:], func=ACT.Exp)
        ident = keep.tile([P, P], F32, name="ident", align_bytes=64)
        make_identity(nc, ident[:])
        mask = keep.tile([P, P], F32, name="mask", align_bytes=64)
        nc.gpsimd.tensor_scalar(out=mask[:], in0=ident[:], scalar1=NEG, scalar2=0.0, op0=ALU.mult, op1=ALU.add)
        nbt = keep.tile([P, P], F32, name="nbt", align_bytes=64)
        nc.gpsimd.memset(nbt[:], 0.0)
        tot = keep.tile([P, P], F32, name="tot", align_bytes=64)
        nc.gpsimd.memset(tot[:], 0.0)
        ibc = keep.tile([P, P], F32, name="ibc", align_bytes=64)
        nc.gpsimd.memset(ibc[:], 0.0)
        beta = keep.tile([P, H], F32, name="beta", align_bytes=64)
        nbeta = keep.tile([P, H], F32, name="nbeta", align_bytes=64)
        ib = keep.tile([P, H], F32, name="ib", align_bytes=64)
        sums = keep.tile([P, 2, 16], F32, name="sums", align_bytes=64)
        ib16 = keep.tile([16, 2], F32, name="ib16", align_bytes=64)

        codes = {}
        bank = {}
        grouped = {}
        xb = {}
        cols = {}
        for b in range(B):
            for h in range(H):
                for m in "kq":
                    cols[b, h, m] = (
                        keep.tile([P, N], U32, name="c%s%d%d" % (m, b, h), align_bytes=256),
                        keep.tile([P, N], U8, name="s%s%d%d" % (m, b, h), align_bytes=256),
                    )

        def mult(b, j):
            t = ring.tile([P, D], BF16, name="xb", align_bytes=64)
            nc.vector.tensor_tensor(out=t[:], in0=xbytes[b, j].bitcast(F8), in1=scale_t[:], op=ALU.mult)
            xb[b, j] = t[:]

        def warm(width):
            ps = psum.tile([P, N], F32, tag="a", name="warmed")
            nc.tensor.matmul(out=ps[:, 0:width], lhsT=wz[:, 0:P], rhs=wz[:, 0:width], start=True, stop=True)

        def turn_scale():
            for c in range(2):
                ps = psum.tile([P, 4, P], F32, tag="z", name="scaled")
                for m in range(4):
                    nc.tensor.transpose(ps[:, m, :], sv[:, c, m : m + 1].to_broadcast([P, P]), ident[:])
                bank["scale%d" % c] = ps

        def take_scale(c, copy):
            dst = scale_t[:, 512 * c : 512 * (c + 1)].rearrange("p (n m) -> p n m", m=4)
            copy(out=dst, in_=bank["scale%d" % c][:].rearrange("p m n -> p n m"))

        def turn_x(key, b, j):
            turn(key, xb[b, j])

        def turn_w(key, m, h, t):
            turn(key, wrows[h, m, t])

        def turn(key, rows):
            ps = psum.tile([P, 4, P], F32, tag="z", name="turned")
            words = rows.bitcast(F32)
            for g in range(PASSES):
                for u in range(2):
                    nc.tensor.transpose(ps[:, 2 * g + u, :], words[:, 256 * g + u : 256 * (g + 1) : 2], ident[:])
            bank[key] = ps

        def take_turn(key, copy):
            g = ring.tile([P, PASSES, P, 4], BF16, name="gt", align_bytes=64)
            dst = g[:].rearrange("p g r e -> p (g r e)").bitcast(F32).rearrange("p (g r u) -> p g r u", g=PASSES, u=2)
            copy(out=dst, in_=bank[key][:].rearrange("p (g u) r -> p g r u", u=2))
            grouped[key] = g

        def quant_turn(key):
            c = keep.tile([P, PASSES, P], U32, name="c_" + key, align_bytes=256)
            s = keep.tile([P, PASSES, P], U8, name="s_" + key, align_bytes=256)
            nc.vector.quantize_mx(
                out=c[:].rearrange("p g r -> p (g r)").bitcast(X4),
                scales=s[:].rearrange("p g r -> p (g r)"),
                in_=grouped[key][:].rearrange("p g r e -> p (g r e)"),
            )
            codes[key] = (c, s)

        def mm_proj(key, b, h, m, j):
            ps = psum.tile([P, 4, P], F32, tag="a", name="proj")
            xc, xs = codes["x%d%d" % (b, j)]
            for t in range(4):
                wc, ws = codes["%s%d%d" % (m, h, t)]
                for g in range(PASSES):
                    nc.tensor.matmul_mx(
                        out=ps[:, t, :], lhsT=wc[:, g, :].bitcast(X4), lhsT_scale=ws[:, g, :],
                        rhs=xc[:, g, :].bitcast(X4), rhs_scale=xs[:, g, :],
                        start=(g == 0), stop=(g == PASSES - 1),
                    )
            bank[key] = ps

        def take_proj(key, on_vector):
            g = ring.tile([P, P, 4], BF16, name="gp", align_bytes=64)
            src = bank[key][:].rearrange("p t n -> p n t")
            if on_vector:
                nc.vector.tensor_copy(out=g[:], in_=src)
            else:
                nc.scalar.copy(out=g[:], in_=src)
            grouped[key] = g

        def quant_proj(key, b, h, m, j):
            c, s = cols[b, h, m]
            nc.vector.quantize_mx(
                out=c[:, j * P : (j + 1) * P].bitcast(X4), scales=s[:, j * P : (j + 1) * P],
                in_=grouped[key][:].rearrange("p n t -> p (n t)"),
            )

        def mm_score(key, b, h, j):
            ps = psum.tile([P, N], F32, tag="z", name="score")
            qc, qs = cols[b, h, "q"]
            kc, ks = cols[b, h, "k"]
            o = j ^ 1
            pair = 2 - 2 * (j // 2)
            for dst, src, w in ((0, j, P), (P, o, P), (2 * P, pair, 2 * P)):
                nc.tensor.matmul_mx(
                    out=ps[:, dst : dst + w],
                    lhsT=qc[:, j * P : (j + 1) * P].bitcast(X4), lhsT_scale=qs[:, j * P : (j + 1) * P],
                    rhs=kc[:, src * P : src * P + w].bitcast(X4), rhs_scale=ks[:, src * P : src * P + w],
                    start=True, stop=True,
                )
            bank[key] = ps

        peaks = {}
        diags = {}

        def hide(key):
            dg = ring.tile([P, P], F32, name="dg", align_bytes=64)
            nc.vector.tensor_tensor(out=dg[:], in0=bank[key][:, 0:P], in1=mask[:], op=ALU.add)
            diags[key] = dg
            peaks[key] = ring.tile([P, 2], F32, name="pk", align_bytes=64)

        def peak_rest(key):
            nc.vector.reduce_max(out=peaks[key][:, 0:1], in_=bank[key][:, P:N], axis=AX.X)

        def peak_diag(key):
            nc.vector.reduce_max(out=peaks[key][:, 1:2], in_=diags[key][:], axis=AX.X)

        def bias(key, h, c):
            pk = peaks[key]
            nc.vector.scalar_tensor_tensor(
                out=nbt[:, c : c + 1], in0=pk[:, 0:1], scalar=pk[:, 1:2], in1=nbeta[:, h : h + 1],
                op0=ALU.max, op1=ALU.mult,
            )

        def exp_rest(key, h, c):
            e1 = ring.tile([P, 3 * P], BF16, name="e1", align_bytes=64)
            nc.scalar.activation(
                out=e1[:], in_=bank[key][:, P:N], func=ACT.Exp, bias=nbt[:, c : c + 1],
                scale=beta[:, h : h + 1], accum_out=sums[:, 0, c : c + 1],
            )

        def exp_diag(key, h, c):
            e2 = ring.tile([P, P], BF16, name="e2", align_bytes=64)
            nc.scalar.activation(
                out=e2[:], in_=diags[key][:], func=ACT.Exp, bias=nbt[:, c : c + 1],
                scale=beta[:, h : h + 1], accum_out=sums[:, 1, c : c + 1],
            )

        def setup_beta():
            nc.vector.tensor_copy(out=beta[:], in_=beta_b[:])
            nc.vector.tensor_scalar(out=nbeta[:], in0=beta[:], scalar1=-1.0, scalar2=None, op0=ALU.mult)
            nc.vector.reciprocal(out=ib[:], in_=beta[:])
            ibv = ibc[:, 0:16].rearrange("p (b h j) -> p b h j", b=B, h=H)
            for h in range(H):
                nc.vector.tensor_scalar(
                    out=ibv[:, :, h, :], in0=ibv[:, :, h, :], scalar1=ib[:, h : h + 1], scalar2=None, op0=ALU.add
                )

        order = ORDER.split()
        proj = [t for t in order if t[0] in "KQ"]
        queues = {"S": [], "V": [], "T": []}

        def add(engine, slot, key, needs, emit, *args):
            queues[engine].append((slot, len(queues[engine]), key, needs, emit, args))

        xs = [t for t in order if t[0] == "x"]
        for i, t in enumerate(order):
            kind, a, c = t[0], int(t[1]), int(t[2])
            if kind in "kqx":
                if kind == "x":
                    n = xs.index(t)
                    add("V", MULT0 + MULT_STEP * n if n < 4 else MULT4 + n - 4, "M" + t, ["scale0", "scale1"], mult, a, c)
                    add("T", i, "T" + t, ["M" + t], turn_x, t, a, c)
                else:
                    add("T", i, "T" + t, [], turn_w, t, kind, a, c)
                if t in ("x11", "x13"):
                    add("V", i + LAG["X"], "X" + t, ["T" + t], take_turn, t, nc.vector.tensor_copy)
                else:
                    add("S", i + LAG["X"], "X" + t, ["T" + t], take_turn, t, nc.scalar.copy)
                add("V", i + LAG["Q"], "Q" + t, ["X" + t], quant_turn, t)
            elif kind in "KQ":
                m, j = {"K": "k", "Q": "q"}[kind], int(t[3])
                needs = ["Qx%d%d" % (a, j)] + ["Q%s%d%d" % (m, c, z) for z in range(4)]
                add("T", i, "T" + t, needs, mm_proj, t, a, c, m, j)
                n = proj.index(t)
                on_vector = V_FIRST <= n < V_LAST and (n - V_FIRST) % V_STEP == 0
                add("V" if on_vector else "S", i + LAG["X"], "X" + t, ["T" + t], take_proj, t, on_vector)
                add("V", i + LAG["Q"], "Q" + t, ["X" + t], quant_proj, t, a, c, m, j)
            else:
                j = int(t[3])
                col = (a * H + c) * TB + j
                needs = ["QQ%d%d%d" % (a, c, j)] + ["QK%d%d%d" % (a, c, z) for z in range(4)]
                add("T", i, "T" + t, needs, mm_score, t, a, c, j)
                add("V", i + LAG["A"], "A" + t, ["T" + t], hide, t)
                add("V", i + LAG["R"], "R" + t, ["T" + t], peak_rest, t)
                add("V", i + LAG["G"], "G" + t, ["A" + t], peak_diag, t)
                add("V", i + LAG["B"], "B" + t, ["R" + t, "G" + t], bias, t, c, col)
                add("S", i + LAG["E"], "E" + t, ["B" + t], exp_rest, t, c, col)
                add("S", i + LAG["F"], "F" + t, ["B" + t], exp_diag, t, c, col)

            if i < WARM_TASKS and kind in "kqx":
                add("T", i + 0.5, "D%d" % i, [], warm, 2 * P)
        for i in range(WARM_START):
            add("T", -1.0, "W%d" % i, [], warm, N)
        add("T", SCALE_SLOT - 0.1, "scale", [], turn_scale)
        add("S", SCALE_SLOT - 0.1, "scale0", ["scale"], take_scale, 0, nc.scalar.copy)
        add("V", SCALE_SLOT - 0.1, "scale1", ["scale", "scale0"], take_scale, 1, nc.vector.tensor_copy)
        add("V", 20.5, "beta", [], setup_beta)
        queues = {e: sorted(queues[e]) for e in "SVT"}
        done = set()
        heads = {"S": 0, "V": 0, "T": 0}
        while any(heads[e] < len(queues[e]) for e in heads):
            moved = False
            for e in "SVT":
                while heads[e] < len(queues[e]):
                    slot, n, key, needs, emit, args = queues[e][heads[e]]
                    if not all(k in done for k in needs):
                        break
                    emit(*args)
                    done.add(key)
                    heads[e] += 1
                    moved = True
                    if e == "T":
                        break
            assert moved

        fin = psum.tile([P, 2, P], F32, tag="a", name="fin")
        nc.tensor.transpose(fin[:, 1, :], ibc[:], ident[:])
        nc.tensor.transpose(fin[:, 0, :], nbt[:], ident[:])
        nc.vector.tensor_copy(out=ib16[:, 0:1], in_=fin[0:16, 1, 0:1])
        nc.vector.tensor_scalar(out=ib16[:, 1:2], in0=fin[0:16, 1, 0:1], scalar1=-1.0, scalar2=None, op0=ALU.mult)
        nc.vector.tensor_tensor(out=tot[:, 0:16], in0=sums[:, 0, :], in1=sums[:, 1, :], op=ALU.add)
        turned = psum.tile([P, P], F32, tag="z", name="turned_tot")
        nc.tensor.transpose(turned[:], tot[:], ident[:])
        pre = keep.tile([16, P], F32, name="pre", align_bytes=64)
        nc.vector.tensor_scalar(out=pre[:], in0=fin[0:16, 0, :], scalar1=ib16[:, 0:1], scalar2=None, op0=ALU.mult)
        ln = keep.tile([16, P], F32, name="ln", align_bytes=64)
        nc.scalar.activation(out=ln[:], in_=turned[0:16, :], func=ACT.Ln)
        res = keep.tile([16, P], F32, name="res", align_bytes=64)
        nc.vector.scalar_tensor_tensor(
            out=res[:], in0=ln[:], scalar=ib16[:, 1:2], in1=pre[:], op0=ALU.mult, op1=ALU.add
        )
        nc.sync.dma_start(out=out.rearrange("b h (j p) -> (b h j) p", p=P), in_=res[:])
